import numpy as np
import ml_dtypes


def mxq(x, axis, fmt="e4m3"):
    dtype, down = {"e4m3": (ml_dtypes.float8_e4m3fn, 7), "e5m2": (ml_dtypes.float8_e5m2, 14)}[fmt]
    v = np.moveaxis(np.asarray(x, np.float32).astype(ml_dtypes.bfloat16).astype(np.float64), axis, -1)
    blocks = v.reshape(v.shape[:-1] + (-1, 32))
    amax = np.abs(blocks).max(-1, keepdims=True)
    byte = np.maximum(np.where(amax > 0, np.frexp(amax)[1] - 1 + 127, 0) - down, 1)
    scale = np.exp2(byte - 127.0)
    codes = (blocks / scale).astype(np.float32).astype(dtype).astype(np.float64)
    return np.moveaxis((codes * scale).reshape(v.shape), -1, axis)


WIDE = False


def mx_kscale(k):
    if not WIDE:
        return np.ones(k)
    levels = np.array([10, -10, 5, -5, 0])
    if k % 512:
        return np.exp2(np.random.permutation(np.resize(levels, k // 32))).repeat(32)
    a = np.empty((k // 512, 16))
    for p in range(k // 512):
        a[p, :8] = np.random.permutation(np.resize(levels, 8))
        for g in range(8):
            far = levels[np.abs(levels - a[p, g]) >= 10]
            a[p, g + 8] = far[np.random.randint(len(far))]
    return np.exp2(a.ravel()).repeat(32)


BF16 = ml_dtypes.bfloat16


def bf(x):
    return np.asarray(x, np.float32).astype(BF16)


def f64(x):
    return np.asarray(x).astype(np.float64)


E2M1 = np.array([0.0, 0.5, 1.0, 1.5, 2.0, 3.0, 4.0, 6.0, -0.0, -0.5, -1.0, -1.5, -2.0, -3.0, -4.0, -6.0])


def pack_weight(w, fmt):
    k, n = w.shape
    w = f64(bf(w)).reshape(k // 32, 32, n)
    amax = np.abs(w).max(1)
    if fmt == "e4m3":
        byte = np.frexp(amax)[1] - 1 + 127 - 7
    else:
        mant, ex = np.frexp(amax / 6.0)
        byte = np.where(mant > 0.5, ex, ex - 1) + 127
    byte = np.clip(np.where(amax > 0, byte, 1), 1, 254)
    scaled = (w * np.exp2(127.0 - byte)[:, None, :]).reshape(k, n).astype(np.float32)
    by_word = np.ascontiguousarray(scaled.reshape(k // 512, 128, 4, n).transpose(0, 1, 3, 2))
    if fmt == "e4m3":
        words = by_word.astype(ml_dtypes.float8_e4m3fn).view(np.uint8)
    else:
        c = by_word.astype(ml_dtypes.float4_e2m1fn).view(np.uint8) & 0xF
        words = c[..., 0::2] | (c[..., 1::2] << 4)
    return np.ascontiguousarray(words), np.ascontiguousarray(byte.astype(np.uint8).reshape(k // 512, 16, n))


def unpack_weight(words, scales, fmt):
    g, p, n, _ = words.shape
    if fmt == "e4m3":
        vals = np.ascontiguousarray(words).view(ml_dtypes.float8_e4m3fn).astype(np.float64)
    else:
        nib = np.empty((g, p, n, 4), np.uint8)
        nib[..., 0::2] = words & 0xF
        nib[..., 1::2] = words >> 4
        vals = E2M1[nib]
    vals = vals * np.repeat(np.exp2(scales.astype(np.float64) - 127.0), 8, axis=1)[..., None]
    return vals.transpose(0, 1, 3, 2).reshape(g * 512, n)
def pack4(w):
    words, scales = pack_weight(w, "e2m1")
    return words.reshape(words.shape[0], 128, -1), scales


def unpack4(words, scales):
    return unpack_weight(words.reshape(words.shape[0], 128, -1, 2), scales, "e2m1")


B, X, N, OS = 2048, 512, 2304, 256
H = N - OS


def draw0():
    s, t = mx_kscale(X), mx_kscale(H)
    std0 = np.sqrt(2.0 / X)
    std1 = np.sqrt(2.0 / (X + H))
    row_scale = np.concatenate([std0 * t, np.full(OS, std1)])
    bias_scale = np.concatenate([t, np.ones(OS)])
    x = bf(np.random.standard_normal((B, X)) * s)
    w0_words, w0_scales = pack4((np.random.standard_normal((N, X)) * row_scale[:, None] / s).T)
    w1_words, w1_scales = pack4((np.random.standard_normal((OS, H)) * std1 / t).T)
    return {"x": x,
            "w0_words": w0_words, "w0_scales": w0_scales,
            "w1_words": w1_words, "w1_scales": w1_scales,
            "biases": bf(np.random.random(N) * bias_scale)}


def core(x, w0_words, w0_scales, w1_words, w1_scales, biases):
    n = w0_scales.shape[2]
    os_ = w1_scales.shape[2]
    z = (mxq(f64(x), 1, "e4m3") @ unpack4(w0_words, w0_scales)) + f64(biases)
    h = np.maximum(z[:, : n - os_], 0.0)
    return z[:, n - os_:] + (mxq(h, 1, "e4m3") @ unpack4(w1_words, w1_scales))


def e4m3fn_bytes(y):
    return np.clip(np.asarray(y, np.float64), -448.0, 448.0).astype(np.float32).astype(ml_dtypes.float8_e4m3fn).view(np.uint8)


def e4m3fn_values(b):
    return np.asarray(b, np.uint8).view(ml_dtypes.float8_e4m3fn).astype(np.float64)


def setup_inputs():
    d = draw0()
    x0 = np.asarray(d['x']).astype(np.float64)
    s = (np.max(np.abs(x0), axis=(0,), keepdims=True) / 448.0).astype(np.float32)
    out = {}
    for k, v in d.items():
        if k == 'x':
            out['x_bytes'] = e4m3fn_bytes(x0 / s.astype(np.float64))
            out['x_scale'] = s
        else:
            out[k] = v
    return out


def reference(x_bytes, x_scale, w0_words, w0_scales, w1_words, w1_scales, biases):
    return core(e4m3fn_values(x_bytes) * x_scale.astype(np.float64), w0_words, w0_scales, w1_words, w1_scales, biases)

@@ -1,0 +1,268 @@
+from contextlib import ExitStack
+
+import concourse.mybir as mybir
+from concourse.masks import make_identity
+
+F32 = mybir.dt.float32
+BF16 = mybir.dt.bfloat16
+U32 = mybir.dt.uint32
+I32 = mybir.dt.int32
+U8 = mybir.dt.uint8
+FP8 = mybir.dt.float8_e4m3fn
+FP8X4 = mybir.dt.float8_e4m3fn_x4
+FP4X4 = mybir.dt.float4_e2m1fn_x4
+RELU = mybir.ActivationFunctionType.Relu
+MULT = mybir.AluOpType.mult
+ADD = mybir.AluOpType.add
+
+P = 128
+B, X, N, OS = 2048, 512, 2304, 256
+H = N - OS
+G = H // 512
+FLOPS = 2 * B * X * N + 2 * B * H * OS
+
+CHUNKS = (2, 4, 4, 4, 2)
+SHARE = (96, 64, 64, 64, 32)
+
+
+def tile_spn_w4_kernel(tc, x_bytes, x_scale, w0_words, w0_scales, w1_words, w1_scales, biases, out):
+    nc = tc.nc
+    n_chunks = len(CHUNKS)
+    first = [sum(CHUNKS[:c]) for c in range(n_chunks)]
+    x_view = x_bytes.rearrange("(p j) k -> p j k", j=B // P)
+    out_view = out.rearrange("(p j) n -> p j n", j=B // P)
+
+    with ExitStack() as ctx:
+        keep = ctx.enter_context(tc.tile_pool(name="keep", bufs=1))
+        work = ctx.enter_context(tc.tile_pool(name="work", bufs=4))
+        psum = ctx.enter_context(tc.psum_pool(name="psum", bufs=5))
+        ctx.enter_context(tc.manual_schedule())
+
+        ident = keep.tile([P, P], F32, name="ident")
+        xs = keep.tile([P, X], F32, name="xs")
+        w0_raw = keep.tile([P, 2 * N], U8, name="w0_raw", align_bytes=64)
+        w0s_raw = keep.tile([P, N], U8, name="w0s_raw", align_bytes=64)
+        w0_perm = keep.tile([P, 2 * H], U8, name="w0_perm", align_bytes=64)
+        w0s_perm = keep.tile([P, H], U8, name="w0s_perm", align_bytes=64)
+        w1 = keep.tile([P, G, 2 * OS], U8, name="w1", align_bytes=64)
+        w1s = keep.tile([P, G, OS], U8, name="w1s", align_bytes=64)
+        bias_h = keep.tile([P, G, 4], BF16, name="bias_h")
+        bias_o = keep.tile([P, OS], BF16, name="bias_o")
+        warm = keep.tile([P, 1], F32, name="warm")
+        xb = []
+        for c in range(n_chunks):
+            xb_c = keep.tile([P, CHUNKS[c], X], U8, name="xbytes%d" % c, align_bytes=64)
+            xb.append(xb_c)
+
+        nc.vector.memset(w0s_raw[:].bitcast(I32), 0)
+        nc.vector.memset(w1s[:].rearrange("p g n -> p (g n)").bitcast(I32), 0)
+        nc.vector.memset(warm[:], 0.0)
+        make_identity(nc, ident[:])
+
+        def load_x(c):
+            nc.sync.dma_start(out=xb[c][:], in_=x_view[:, first[c] : first[c] + CHUNKS[c], :])
+
+        nc.scalar.dma_start(out=xs[:], in_=x_scale.rearrange("o k -> (o k)").partition_broadcast(P))
+        nc.sync.dma_start(out=w0_raw[:, 0:1024], in_=w0_words[0, :, 0:1024])
+        load_x(0)
+        for q in range(4):
+            nc.sync.dma_start(
+                out=w0s_raw[32 * q : 32 * q + 4, :].bitcast(I32),
+                in_=w0_scales[0, 4 * q : 4 * q + 4, :].bitcast(I32),
+            )
+        nc.scalar.dma_start(out=bias_h[:], in_=biases[0:H].rearrange("(g p t) -> p g t", g=G, p=P, t=4))
+        nc.sync.dma_start(out=w0_raw[:, 1024:2048], in_=w0_words[0, :, 1024:2048])
+        load_x(1)
+        nc.sync.dma_start(out=w0_raw[:, 2048:4608], in_=w0_words[0, :, 2048:4608])
+        nc.sync.dma_start(out=w1[:], in_=w1_words.rearrange("g p n -> p g n"))
+        for q in range(4):
+            nc.sync.dma_start(
+                out=w1s[32 * q : 32 * q + 4].bitcast(I32),
+                in_=w1_scales[:, 4 * q : 4 * q + 4, :].rearrange("g r n -> r g n").bitcast(I32),
+            )
+        nc.scalar.dma_start(out=bias_o[:], in_=biases[H:N].partition_broadcast(P))
+        for c in range(2, n_chunks):
+            load_x(c)
+        nc.scalar.activation(out=warm[:], in_=warm[:], func=RELU)
+
+        xv, xg, xq, xqs = {}, {}, {}, {}
+        xt = {}
+        hp, hg, hq, hqs, acc = {}, {}, {}, {}, {}
+
+        def permute_codes(g):
+            nc.vector.tensor_copy(
+                out=w0_perm[:, 1024 * g : 1024 * (g + 1)].rearrange("p (t m b) -> p t m b", t=4, b=2),
+                in_=w0_raw[:, 1024 * g : 1024 * (g + 1)].rearrange("p (m t b) -> p t m b", t=4, b=2),
+            )
+
+        def permute_scales(g):
+            nc.vector.tensor_copy(
+                out=w0s_perm[:, 512 * g : 512 * (g + 1)].rearrange("p (t m) -> p t m", t=4),
+                in_=w0s_raw[:, 512 * g : 512 * (g + 1)].rearrange("p (m t) -> p t m", t=4),
+            )
+
+        def x_mult(c, j):
+            t = work.tile([P, X], BF16, name="xv", bufs=8, align_bytes=64)
+            xv[c, j] = t
+            nc.vector.tensor_tensor(out=t[:], in0=xb[c][:, j, :].bitcast(FP8), in1=xs[:], op=MULT)
+
+        def x_transpose(c, pair):
+            t = psum.tile([P, 2, 2, P], F32, name="xt", tag="xo", bufs=3)
+            xt[c, pair] = t
+            for jj in range(2):
+                words = xv[c, 2 * pair + jj][:].bitcast(F32)
+                for u in range(2):
+                    nc.tensor.transpose(t[:, jj, u, :], words[:, u : X // 2 : 2], ident[:])
+
+        def x_copy(c, pair):
+            if pair == 0:
+                xg[c] = work.tile([P, 2048], BF16, name="xg", bufs=2, align_bytes=64)
+            nc.scalar.copy(
+                out=xg[c][:, 1024 * pair : 1024 * (pair + 1)].bitcast(F32).rearrange("p (j r u) -> p j r u", j=2, u=2),
+                in_=xt[c, pair][:].rearrange("p j u r -> p j r u"),
+            )
+
+        def x_quantize(c):
+            n = CHUNKS[c] * P
+            xq[c] = work.tile([P, 512], U32, name="xq", bufs=n_chunks, align_bytes=64)
+            xqs[c] = work.tile([P, 512], U8, name="xqs", bufs=n_chunks, align_bytes=64)
+            nc.vector.quantize_mx(out=xq[c][:, :n].bitcast(FP8X4), scales=xqs[c][:, :n], in_=xg[c][:, : 4 * n])
+
+        def stage1(c, g):
+            n = CHUNKS[c] * P
+            h = work.tile([P, 4, 512], BF16, name="hp", bufs=4, align_bytes=64)
+            hp[c, g] = h
+            for t in range(4):
+                z = psum.tile([P, 512], F32, name="z", bufs=5)
+                m0 = 512 * g + P * t
+                nc.tensor.matmul_mx(
+                    out=z[:, :n],
+                    lhsT=w0_perm[:, 2 * m0 : 2 * (m0 + P)].bitcast(FP4X4),
+                    lhsT_scale=w0s_perm[:, m0 : m0 + P],
+                    rhs=xq[c][:, :n].bitcast(FP8X4),
+                    rhs_scale=xqs[c][:, :n],
+                    start=True,
+                    stop=True,
+                )
+                nc.scalar.activation(out=h[:, t, :n], in_=z[:, :n], func=RELU, bias=bias_h[:, g, t : t + 1])
+            hg[c, g] = work.tile([P, 2048], BF16, name="hg", bufs=4, align_bytes=64)
+            weave(nc.scalar.copy, c, g, n - SHARE[c], n)
+
+        def weave(engine_copy, c, g, a, b):
+            if b > a:
+                engine_copy(
+                    out=hg[c, g][:, 4 * a : 4 * b].rearrange("p (n t) -> p n t", t=4),
+                    in_=hp[c, g][:, :, a:b].rearrange("p t n -> p n t"),
+                )
+
+        def h_quantize(c, g, half):
+            n = CHUNKS[c] * P // 2
+            if half == 0:
+                hq[c, g] = work.tile([P, 512], U32, name="hq", bufs=10, align_bytes=64)
+                hqs[c, g] = work.tile([P, 512], U8, name="hqs", bufs=10, align_bytes=64)
+            a = half * n
+            nc.vector.quantize_mx(
+                out=hq[c, g][:, a : a + n].bitcast(FP8X4),
+                scales=hqs[c, g][:, a : a + n],
+                in_=hg[c, g][:, 4 * a : 4 * (a + n)],
+            )
+
+        def stage2(c, j0, count):
+            o = psum.tile([P, 2, OS], F32, name="o", tag="xo", bufs=3)
+            acc[c, j0] = o
+            for jj in range(count):
+                cols = slice((j0 + jj) * P, (j0 + jj + 1) * P)
+                for half in range(2):
+                    dst = o[:, jj, half * P : (half + 1) * P]
+                    n0 = H + half * P
+                    nc.tensor.matmul_mx(
+                        out=dst,
+                        lhsT=xq[c][:, cols].bitcast(FP8X4),
+                        lhsT_scale=xqs[c][:, cols],
+                        rhs=w0_raw[:, 2 * n0 : 2 * (n0 + P)].bitcast(FP4X4),
+                        rhs_scale=w0s_raw[:, n0 : n0 + P],
+                        start=True,
+                        stop=False,
+                    )
+                    for g in range(G):
+                        nc.tensor.matmul_mx(
+                            out=dst,
+                            lhsT=hq[c, g][:, cols].bitcast(FP8X4),
+                            lhsT_scale=hqs[c, g][:, cols],
+                            rhs=w1[:, g, 2 * half * P : 2 * (half + 1) * P].bitcast(FP4X4),
+                            rhs_scale=w1s[:, g, half * P : (half + 1) * P],
+                            start=False,
+                            stop=(g == G - 1),
+                        )
+
+        def finish(c, j0, count):
+            res = work.tile([P, 2, OS], F32, name="res", bufs=4)
+            nc.vector.tensor_tensor(
+                out=res[:, :count, :],
+                in0=acc[c, j0][:, :count, :],
+                in1=bias_o[:].unsqueeze(1).to_broadcast([P, count, OS]),
+                op=ADD,
+            )
+            nc.sync.dma_start(out=out_view[:, first[c] + j0 : first[c] + j0 + count, :], in_=res[:, :count, :])
+
+        permute_codes(0)
+        for j in range(CHUNKS[0]):
+            x_mult(0, j)
+        permute_scales(0)
+        x_transpose(0, 0)
+        x_copy(0, 0)
+        permute_codes(1)
+        x_quantize(0)
+        permute_scales(1)
+        x_mult(1, 0)
+        x_mult(1, 1)
+
+        n_units = n_chunks * G
+        fill = {}
+
+        def put(s, f, *args):
+            fill.setdefault(s, []).append((f, args))
+
+        put(0, permute_codes, 2)
+        put(0, permute_scales, 2)
+        put(1, permute_codes, 3)
+        put(1, permute_scales, 3)
+        for c in range(1, n_chunks):
+            for j in range(CHUNKS[c]):
+                if c > 1 or j > 1:
+                    put(max(4 * (c - 1) - 1 + j // 2, 0), x_mult, c, j)
+            put(4 * (c - 1) + 3, x_quantize, c)
+        for c in range(n_chunks - 1):
+            for i in range(CHUNKS[c] // 2):
+                put(4 * (c + 1) + 3 + i, finish, c, 2 * i, 2)
+
+        for s in range(n_units + 1):
+            fills = fill.get(s, [])
+            if s < n_units:
+                c, g = s // G, s % G
+                stage1(c, g)
+            if s > 0:
+                pc, pg = (s - 1) // G, (s - 1) % G
+                n = CHUNKS[pc] * P
+                share = SHARE[pc]
+                weave(nc.vector.tensor_copy, pc, pg, 0, n // 2)
+                weave(nc.vector.tensor_copy, pc, pg, n // 2, n - share)
+            for f, args in fills[: len(fills) // 2]:
+                f(*args)
+            if s > 0:
+                h_quantize(pc, pg, 0)
+                h_quantize(pc, pg, 1)
+            for f, args in fills[len(fills) // 2 :]:
+                f(*args)
+            if s < n_units:
+                if g == 1 and c + 1 < n_chunks:
+                    for pair in range(CHUNKS[c + 1] // 2):
+                        x_transpose(c + 1, pair)
+                        x_copy(c + 1, pair)
+                if g >= 2 and c > 0 and 2 * (g - 2) < CHUNKS[c - 1]:
+                    stage2(c - 1, 2 * (g - 2), 2)
+
+        last = n_chunks - 1
+        for j in range(CHUNKS[last]):
+            stage2(last, j, 1)
+            finish(last, j, 1)

@@ -22,7 +22,13 @@ G = H // 512
 FLOPS = 2 * B * X * N + 2 * B * H * OS
 
 CHUNKS = (2, 4, 4, 4, 2)
-SHARE = (96, 64, 64, 64, 32)
+SHARE = (16, 0, 0, 0, 48)
+
+
+PERM = (-2, -2, -1, 0)
+XM = (7, 7, 6, 6)
+XT = 3
+XQ = 2
 
 
 def tile_spn_w4_kernel(tc, x_bytes, x_scale, w0_words, w0_scales, w1_words, w1_scales, biases, out):
@@ -48,6 +54,7 @@ def tile_spn_w4_kernel(tc, x_bytes, x_scale, w0_words, w0_scales, w1_words, w1_s
         w1s = keep.tile([P, G, OS], U8, name="w1s", align_bytes=64)
         bias_h = keep.tile([P, G, 4], BF16, name="bias_h")
         bias_o = keep.tile([P, OS], BF16, name="bias_o")
+        xs_col = keep.tile([P, 4], F32, name="xs_col")
         warm = keep.tile([P, 1], F32, name="warm")
         xb = []
         for c in range(n_chunks):
@@ -62,7 +69,7 @@ def tile_spn_w4_kernel(tc, x_bytes, x_scale, w0_words, w0_scales, w1_words, w1_s
         def load_x(c):
             nc.sync.dma_start(out=xb[c][:], in_=x_view[:, first[c] : first[c] + CHUNKS[c], :])
 
-        nc.scalar.dma_start(out=xs[:], in_=x_scale.rearrange("o k -> (o k)").partition_broadcast(P))
+        nc.sync.dma_start(out=xs_col[:], in_=x_scale.rearrange("o (n m) -> n (o m)", m=4))
         nc.sync.dma_start(out=w0_raw[:, 0:1024], in_=w0_words[0, :, 0:1024])
         load_x(0)
         for q in range(4):
@@ -80,9 +87,9 @@ def tile_spn_w4_kernel(tc, x_bytes, x_scale, w0_words, w0_scales, w1_words, w1_s
                 out=w1s[32 * q : 32 * q + 4].bitcast(I32),
                 in_=w1_scales[:, 4 * q : 4 * q + 4, :].rearrange("g r n -> r g n").bitcast(I32),
             )
-        nc.scalar.dma_start(out=bias_o[:], in_=biases[H:N].partition_broadcast(P))
         for c in range(2, n_chunks):
             load_x(c)
+        nc.sync.dma_start(out=bias_o[:], in_=biases[H:N].partition_broadcast(P))
         nc.scalar.activation(out=warm[:], in_=warm[:], func=RELU)
 
         xv, xg, xq, xqs = {}, {}, {}, {}
@@ -151,8 +158,8 @@ def tile_spn_w4_kernel(tc, x_bytes, x_scale, w0_words, w0_scales, w1_words, w1_s
         def weave(engine_copy, c, g, a, b):
             if b > a:
                 engine_copy(
-                    out=hg[c, g][:, 4 * a : 4 * b].rearrange("p (n t) -> p n t", t=4),
-                    in_=hp[c, g][:, :, a:b].rearrange("p t n -> p n t"),
+                    out=hg[c, g][:, 4 * a : 4 * b].rearrange("p (c i t) -> p c t i", t=4, i=4),
+                    in_=hp[c, g][:, :, a:b].rearrange("p t (c i) -> p c t i", i=4),
                 )
 
         def h_quantize(c, g, half):
@@ -205,62 +212,59 @@ def tile_spn_w4_kernel(tc, x_bytes, x_scale, w0_words, w0_scales, w1_words, w1_s
             )
             nc.sync.dma_start(out=out_view[:, first[c] + j0 : first[c] + j0 + count, :], in_=res[:, :count, :])
 
+        n_units = n_chunks * G
+        vec, mid, ten = {}, {}, {}
+
+        def put(table, s, f, *args):
+            table.setdefault(s, []).append((f, args))
+
+        def run(table, s):
+            for f, args in table.get(s, []):
+                f(*args)
+
+        for g in range(1, G):
+            put(vec, PERM[g], permute_codes, g)
+            put(vec, PERM[g], permute_scales, g)
+        for c in range(1, n_chunks):
+            for j in range(CHUNKS[c]):
+                put(vec, max(4 * c - XM[j], -1), x_mult, c, j)
+            for pair in range(CHUNKS[c] // 2):
+                put(ten, 4 * c - XT, x_transpose, c, pair)
+                put(ten, 4 * c - XT, x_copy, c, pair)
+            put(mid, 4 * c - XQ, x_quantize, c)
+        for c in range(n_chunks - 1):
+            for i in range(CHUNKS[c] // 2):
+                put(ten, 4 * (c + 1) + 2 + i, stage2, c, 2 * i, 2)
+                put(mid, 4 * (c + 1) + 3 + i, finish, c, 2 * i, 2)
+
+        spread = psum.tile([P, 4, P], F32, name="spread", tag="xo", bufs=3)
+        for m in range(4):
+            nc.tensor.transpose(spread[:, m, :], xs_col[:, m : m + 1].to_broadcast([P, P]), ident[:])
+        nc.scalar.copy(out=xs[:].rearrange("p (n m) -> p n m", m=4), in_=spread[:].rearrange("p m n -> p n m"))
         permute_codes(0)
         for j in range(CHUNKS[0]):
             x_mult(0, j)
         permute_scales(0)
         x_transpose(0, 0)
         x_copy(0, 0)
-        permute_codes(1)
+        run(vec, -2)
         x_quantize(0)
-        permute_scales(1)
-        x_mult(1, 0)
-        x_mult(1, 1)
-
-        n_units = n_chunks * G
-        fill = {}
-
-        def put(s, f, *args):
-            fill.setdefault(s, []).append((f, args))
-
-        put(0, permute_codes, 2)
-        put(0, permute_scales, 2)
-        put(1, permute_codes, 3)
-        put(1, permute_scales, 3)
-        for c in range(1, n_chunks):
-            for j in range(CHUNKS[c]):
-                if c > 1 or j > 1:
-                    put(max(4 * (c - 1) - 1 + j // 2, 0), x_mult, c, j)
-            put(4 * (c - 1) + 3, x_quantize, c)
-        for c in range(n_chunks - 1):
-            for i in range(CHUNKS[c] // 2):
-                put(4 * (c + 1) + 3 + i, finish, c, 2 * i, 2)
+        run(vec, -1)
 
         for s in range(n_units + 1):
-            fills = fill.get(s, [])
             if s < n_units:
-                c, g = s // G, s % G
-                stage1(c, g)
+                stage1(s // G, s % G)
+                run(ten, s)
             if s > 0:
-                pc, pg = (s - 1) // G, (s - 1) % G
-                n = CHUNKS[pc] * P
-                share = SHARE[pc]
-                weave(nc.vector.tensor_copy, pc, pg, 0, n // 2)
-                weave(nc.vector.tensor_copy, pc, pg, n // 2, n - share)
-            for f, args in fills[: len(fills) // 2]:
-                f(*args)
+                c, g = (s - 1) // G, (s - 1) % G
+                n = CHUNKS[c] * P
+                weave(nc.vector.tensor_copy, c, g, 0, n // 2)
+                weave(nc.vector.tensor_copy, c, g, n // 2, n - SHARE[c])
+            run(mid, s)
             if s > 0:
-                h_quantize(pc, pg, 0)
-                h_quantize(pc, pg, 1)
-            for f, args in fills[len(fills) // 2 :]:
-                f(*args)
-            if s < n_units:
-                if g == 1 and c + 1 < n_chunks:
-                    for pair in range(CHUNKS[c + 1] // 2):
-                        x_transpose(c + 1, pair)
-                        x_copy(c + 1, pair)
-                if g >= 2 and c > 0 and 2 * (g - 2) < CHUNKS[c - 1]:
-                    stage2(c - 1, 2 * (g - 2), 2)
+                h_quantize(c, g, 0)
+                h_quantize(c, g, 1)
+            run(vec, s)
 
         last = n_chunks - 1
         for j in range(CHUNKS[last]):

@@ -22,13 +22,16 @@ G = H // 512
 FLOPS = 2 * B * X * N + 2 * B * H * OS
 
 CHUNKS = (2, 4, 4, 4, 2)
-SHARE = (16, 0, 0, 0, 48)
-
-
-PERM = (-2, -2, -1, 0)
-XM = (7, 7, 6, 6)
-XT = 3
-XQ = 2
+UNITS = tuple((c, g) for c in range(5) for g in range(4))
+SHARE = ((64, 48, 128, 64), (0, 0, 0, 0), (0, 0, 0, 0), (0, 0, 0, 0), (64, 64, 64, 64))
+VE = ((1, 1),)
+CE = 0
+VX = ((0, 0), (2, 0), (3, 0))
+XM = ((), (0, 0, 0, 1), (0, 2, 3, 3), (3, 6, 5, 6), (4, 5))
+XT = (0, 2, 4, 9, 8)
+XQ = (0, 3, 5, 10, 9)
+S2 = ((10,), (11, 12), (14, 17), (18, 19))
+PERM = (-2, -2, -2, -2)
 
 
 def tile_spn_w4_kernel(tc, x_bytes, x_scale, w0_words, w0_scales, w1_words, w1_scales, biases, out):
@@ -69,9 +72,10 @@ def tile_spn_w4_kernel(tc, x_bytes, x_scale, w0_words, w0_scales, w1_words, w1_s
         def load_x(c):
             nc.sync.dma_start(out=xb[c][:], in_=x_view[:, first[c] : first[c] + CHUNKS[c], :])
 
+        load_x(0)
         nc.sync.dma_start(out=xs_col[:], in_=x_scale.rearrange("o (n m) -> n (o m)", m=4))
         nc.sync.dma_start(out=w0_raw[:, 0:1024], in_=w0_words[0, :, 0:1024])
-        load_x(0)
+        load_x(1)
         for q in range(4):
             nc.sync.dma_start(
                 out=w0s_raw[32 * q : 32 * q + 4, :].bitcast(I32),
@@ -79,7 +83,6 @@ def tile_spn_w4_kernel(tc, x_bytes, x_scale, w0_words, w0_scales, w1_words, w1_s
             )
         nc.scalar.dma_start(out=bias_h[:], in_=biases[0:H].rearrange("(g p t) -> p g t", g=G, p=P, t=4))
         nc.sync.dma_start(out=w0_raw[:, 1024:2048], in_=w0_words[0, :, 1024:2048])
-        load_x(1)
         nc.sync.dma_start(out=w0_raw[:, 2048:4608], in_=w0_words[0, :, 2048:4608])
         nc.sync.dma_start(out=w1[:], in_=w1_words.rearrange("g p n -> p g n"))
         for q in range(4):
@@ -113,10 +116,25 @@ def tile_spn_w4_kernel(tc, x_bytes, x_scale, w0_words, w0_scales, w1_words, w1_s
             xv[c, j] = t
             nc.vector.tensor_tensor(out=t[:], in0=xb[c][:, j, :].bitcast(FP8), in1=xs[:], op=MULT)
 
+        def x_cast(c, j):
+            t = work.tile([P, X], BF16, name="xv", bufs=8, align_bytes=64)
+            xv[c, j] = t
+            (nc.scalar.copy if CE else nc.vector.tensor_copy)(out=t[:], in_=xb[c][:, j, :].bitcast(FP8))
+
+        def x_scale_out(c, j):
+            if j == 0:
+                xg[c] = work.tile([P, 2048], BF16, name="xg", bufs=2, align_bytes=64)
+            nc.vector.tensor_tensor(
+                out=xg[c][:, 512 * j : 512 * (j + 1)].rearrange("p (r u e) -> p r u e", u=2, e=2),
+                in0=xt[c, j // 2][:, j % 2].rearrange("p u r -> p (u r)").bitcast(BF16).rearrange("p (u r e) -> p r u e", u=2, e=2),
+                in1=xs_col[:].rearrange("p (o u e) -> p o u e", o=1, u=2).to_broadcast([P, P, 2, 2]),
+                op=MULT,
+            )
+
         def x_transpose(c, pair):
             t = psum.tile([P, 2, 2, P], F32, name="xt", tag="xo", bufs=3)
             xt[c, pair] = t
-            for jj in range(2):
+            for jj in range(min(2, CHUNKS[c] - 2 * pair)):
                 words = xv[c, 2 * pair + jj][:].bitcast(F32)
                 for u in range(2):
                     nc.tensor.transpose(t[:, jj, u, :], words[:, u : X // 2 : 2], ident[:])
@@ -124,9 +142,11 @@ def tile_spn_w4_kernel(tc, x_bytes, x_scale, w0_words, w0_scales, w1_words, w1_s
         def x_copy(c, pair):
             if pair == 0:
                 xg[c] = work.tile([P, 2048], BF16, name="xg", bufs=2, align_bytes=64)
-            nc.scalar.copy(
-                out=xg[c][:, 1024 * pair : 1024 * (pair + 1)].bitcast(F32).rearrange("p (j r u) -> p j r u", j=2, u=2),
-                in_=xt[c, pair][:].rearrange("p j u r -> p j r u"),
+            k = min(2, CHUNKS[c] - 2 * pair)
+            move = nc.vector.tensor_copy if (c, pair) in VX else nc.scalar.copy
+            move(
+                out=xg[c][:, 1024 * pair : 1024 * pair + 512 * k].bitcast(F32).rearrange("p (j r u) -> p j r u", j=k, u=2),
+                in_=xt[c, pair][:, :k].rearrange("p j u r -> p j r u"),
             )
 
         def x_quantize(c):
@@ -151,9 +171,12 @@ def tile_spn_w4_kernel(tc, x_bytes, x_scale, w0_words, w0_scales, w1_words, w1_s
                     start=True,
                     stop=True,
                 )
-                nc.scalar.activation(out=h[:, t, :n], in_=z[:, :n], func=RELU, bias=bias_h[:, g, t : t + 1])
+                if t == 3 and (c, g) in VE:
+                    nc.vector.tensor_scalar(out=h[:, t, :n], in0=z[:, :n], scalar1=bias_h[:, g, t : t + 1], scalar2=0.0, op0=ADD, op1=mybir.AluOpType.max)
+                else:
+                    nc.scalar.activation(out=h[:, t, :n], in_=z[:, :n], func=RELU, bias=bias_h[:, g, t : t + 1])
             hg[c, g] = work.tile([P, 2048], BF16, name="hg", bufs=4, align_bytes=64)
-            weave(nc.scalar.copy, c, g, n - SHARE[c], n)
+            weave(nc.scalar.copy, c, g, n - SHARE[c][g], n)
 
         def weave(engine_copy, c, g, a, b):
             if b > a:
@@ -163,10 +186,10 @@ def tile_spn_w4_kernel(tc, x_bytes, x_scale, w0_words, w0_scales, w1_words, w1_s
                 )
 
         def h_quantize(c, g, half):
-            n = CHUNKS[c] * P // 2
+            n = CHUNKS[c] * P // halves[c]
             if half == 0:
-                hq[c, g] = work.tile([P, 512], U32, name="hq", bufs=10, align_bytes=64)
-                hqs[c, g] = work.tile([P, 512], U8, name="hqs", bufs=10, align_bytes=64)
+                hq[c, g] = work.tile([P, 512], U32, name="hq", bufs=12, align_bytes=64)
+                hqs[c, g] = work.tile([P, 512], U8, name="hqs", bufs=12, align_bytes=64)
             a = half * n
             nc.vector.quantize_mx(
                 out=hq[c, g][:, a : a + n].bitcast(FP8X4),
@@ -174,33 +197,36 @@ def tile_spn_w4_kernel(tc, x_bytes, x_scale, w0_words, w0_scales, w1_words, w1_s
                 in_=hg[c, g][:, 4 * a : 4 * (a + n)],
             )
 
+        def pass2(dst, c, j, half, opens, groups, closes):
+            cols = slice(j * P, (j + 1) * P)
+            n0 = H + half * P
+            if opens:
+                nc.tensor.matmul_mx(
+                    out=dst,
+                    lhsT=xq[c][:, cols].bitcast(FP8X4),
+                    lhsT_scale=xqs[c][:, cols],
+                    rhs=w0_raw[:, 2 * n0 : 2 * (n0 + P)].bitcast(FP4X4),
+                    rhs_scale=w0s_raw[:, n0 : n0 + P],
+                    start=True,
+                    stop=False,
+                )
+            for g in groups:
+                nc.tensor.matmul_mx(
+                    out=dst,
+                    lhsT=hq[c, g][:, cols].bitcast(FP8X4),
+                    lhsT_scale=hqs[c, g][:, cols],
+                    rhs=w1[:, g, 2 * half * P : 2 * (half + 1) * P].bitcast(FP4X4),
+                    rhs_scale=w1s[:, g, half * P : (half + 1) * P],
+                    start=False,
+                    stop=(closes and g == groups[-1]),
+                )
+
         def stage2(c, j0, count):
             o = psum.tile([P, 2, OS], F32, name="o", tag="xo", bufs=3)
             acc[c, j0] = o
             for jj in range(count):
-                cols = slice((j0 + jj) * P, (j0 + jj + 1) * P)
                 for half in range(2):
-                    dst = o[:, jj, half * P : (half + 1) * P]
-                    n0 = H + half * P
-                    nc.tensor.matmul_mx(
-                        out=dst,
-                        lhsT=xq[c][:, cols].bitcast(FP8X4),
-                        lhsT_scale=xqs[c][:, cols],
-                        rhs=w0_raw[:, 2 * n0 : 2 * (n0 + P)].bitcast(FP4X4),
-                        rhs_scale=w0s_raw[:, n0 : n0 + P],
-                        start=True,
-                        stop=False,
-                    )
-                    for g in range(G):
-                        nc.tensor.matmul_mx(
-                            out=dst,
-                            lhsT=hq[c, g][:, cols].bitcast(FP8X4),
-                            lhsT_scale=hqs[c, g][:, cols],
-                            rhs=w1[:, g, 2 * half * P : 2 * (half + 1) * P].bitcast(FP4X4),
-                            rhs_scale=w1s[:, g, half * P : (half + 1) * P],
-                            start=False,
-                            stop=(g == G - 1),
-                        )
+                    pass2(o[:, jj, half * P : (half + 1) * P], c, j0 + jj, half, True, range(G), True)
 
         def finish(c, j0, count):
             res = work.tile([P, 2, OS], F32, name="res", bufs=4)
@@ -212,7 +238,29 @@ def tile_spn_w4_kernel(tc, x_bytes, x_scale, w0_words, w0_scales, w1_words, w1_s
             )
             nc.sync.dma_start(out=out_view[:, first[c] + j0 : first[c] + j0 + count, :], in_=res[:, :count, :])
 
-        n_units = n_chunks * G
+        last = n_chunks - 1
+        tail = {}
+
+        def open_last():
+            for j in range(CHUNKS[last]):
+                for half in range(2):
+                    tag, bufs = ("xo", 3) if j == 0 else ("z", 5)
+                    o = psum.tile([P, P], F32, name="tail", tag=tag, bufs=bufs)
+                    tail[j, half] = o
+                    pass2(o[:], last, j, half, True, range(G - 1), False)
+
+        def close_last(j):
+            for half in range(2):
+                pass2(tail[j, half][:], last, j, half, False, (G - 1,), True)
+
+        def finish_last(j):
+            res = work.tile([P, OS], F32, name="tail_res", bufs=2)
+            for half in range(2):
+                cols = slice(half * P, (half + 1) * P)
+                nc.vector.tensor_tensor(out=res[:, cols], in0=tail[j, half][:], in1=bias_o[:, cols], op=ADD)
+            nc.sync.dma_start(out=out_view[:, first[last] + j, :], in_=res[:])
+
+        n_units = len(UNITS)
         vec, mid, ten = {}, {}, {}
 
         def put(table, s, f, *args):
@@ -222,51 +270,57 @@ def tile_spn_w4_kernel(tc, x_bytes, x_scale, w0_words, w0_scales, w1_words, w1_s
             for f, args in table.get(s, []):
                 f(*args)
 
+        halves = [1 if r == 1 else 2 for r in CHUNKS]
+        pairs = [(r + 1) // 2 for r in CHUNKS]
         for g in range(1, G):
             put(vec, PERM[g], permute_codes, g)
             put(vec, PERM[g], permute_scales, g)
         for c in range(1, n_chunks):
             for j in range(CHUNKS[c]):
-                put(vec, max(4 * c - XM[j], -1), x_mult, c, j)
-            for pair in range(CHUNKS[c] // 2):
-                put(ten, 4 * c - XT, x_transpose, c, pair)
-                put(ten, 4 * c - XT, x_copy, c, pair)
-            put(mid, 4 * c - XQ, x_quantize, c)
-        for c in range(n_chunks - 1):
-            for i in range(CHUNKS[c] // 2):
-                put(ten, 4 * (c + 1) + 2 + i, stage2, c, 2 * i, 2)
-                put(mid, 4 * (c + 1) + 3 + i, finish, c, 2 * i, 2)
+                put(vec, XM[c][j], x_mult, c, j)
+            for pair in range(pairs[c]):
+                put(ten, XT[c], x_transpose, c, pair)
+                put(ten, XT[c], x_copy, c, pair)
+            put(mid, XQ[c], x_quantize, c)
+        for c in range(last):
+            for i in range(pairs[c]):
+                k = min(2, CHUNKS[c] - 2 * i)
+                put(ten, S2[c][i], stage2, c, 2 * i, k)
+                put(vec if c == last - 1 else mid, S2[c][i] + 1, finish, c, 2 * i, k)
+        put(ten, n_units, open_last)
 
+        for j in range(CHUNKS[0]):
+            x_cast(0, j)
+        x_transpose(0, 0)
         spread = psum.tile([P, 4, P], F32, name="spread", tag="xo", bufs=3)
         for m in range(4):
             nc.tensor.transpose(spread[:, m, :], xs_col[:, m : m + 1].to_broadcast([P, P]), ident[:])
         nc.scalar.copy(out=xs[:].rearrange("p (n m) -> p n m", m=4), in_=spread[:].rearrange("p m n -> p n m"))
         permute_codes(0)
         for j in range(CHUNKS[0]):
-            x_mult(0, j)
+            x_scale_out(0, j)
         permute_scales(0)
-        x_transpose(0, 0)
-        x_copy(0, 0)
-        run(vec, -2)
         x_quantize(0)
+        run(vec, -2)
         run(vec, -1)
 
         for s in range(n_units + 1):
             if s < n_units:
-                stage1(s // G, s % G)
-                run(ten, s)
+                stage1(*UNITS[s])
             if s > 0:
-                c, g = (s - 1) // G, (s - 1) % G
+                c, g = UNITS[s - 1]
                 n = CHUNKS[c] * P
-                weave(nc.vector.tensor_copy, c, g, 0, n // 2)
-                weave(nc.vector.tensor_copy, c, g, n // 2, n - SHARE[c])
+                cut = n // halves[c]
+                end = n - SHARE[c][g]
+                weave(nc.vector.tensor_copy, c, g, 0, min(cut, end))
+                weave(nc.vector.tensor_copy, c, g, cut, end)
             run(mid, s)
             if s > 0:
                 h_quantize(c, g, 0)
-                h_quantize(c, g, 1)
+                if halves[c] == 2:
+                    h_quantize(c, g, 1)
+            run(ten, s)
             run(vec, s)
-
-        last = n_chunks - 1
         for j in range(CHUNKS[last]):
-            stage2(last, j, 1)
-            finish(last, j, 1)
+            close_last(j)
+            finish_last(j)

@@ -23,15 +23,19 @@ FLOPS = 2 * B * X * N + 2 * B * H * OS
 
 CHUNKS = (2, 4, 4, 4, 2)
 UNITS = tuple((c, g) for c in range(5) for g in range(4))
-SHARE = ((64, 48, 128, 64), (0, 0, 0, 0), (0, 0, 0, 0), (0, 0, 0, 0), (64, 64, 64, 64))
-VE = ((1, 1),)
+SHARE = ((48, 48, 48, 48), (0, 0, 0, 0), (0, 0, 0, 0), (0, 0, 0, 0), (48, 48, 48, 48))
+VE = ((3, 3),)
 CE = 0
-VX = ((0, 0), (2, 0), (3, 0))
-XM = ((), (0, 0, 0, 1), (0, 2, 3, 3), (3, 6, 5, 6), (4, 5))
-XT = (0, 2, 4, 9, 8)
-XQ = (0, 3, 5, 10, 9)
-S2 = ((10,), (11, 12), (14, 17), (18, 19))
-PERM = (-2, -2, -2, -2)
+VX = ()
+SC = (0, 1)
+SP = 1
+OL = (20, 20)
+WARM = (5, 3)
+XM = ((), (0, 0, 0, 0), (2, 2, 3, 3), (6, 6, 7, 7), (10, 10))
+XT = (0, 0, 5, 9, 13)
+XQ = (0, 1, 6, 10, 14)
+S2 = ((6,), (10, 11), (14, 15), (18, 19))
+PERM = (-2, -2, -2, -1)
 
 
 def tile_spn_w4_kernel(tc, x_bytes, x_scale, w0_words, w0_scales, w1_words, w1_scales, biases, out):
@@ -64,6 +68,8 @@ def tile_spn_w4_kernel(tc, x_bytes, x_scale, w0_words, w0_scales, w1_words, w1_s
             xb_c = keep.tile([P, CHUNKS[c], X], U8, name="xbytes%d" % c, align_bytes=64)
             xb.append(xb_c)
 
+        zeros = keep.tile([P, 512], BF16, name="zeros")
+        nc.vector.memset(zeros[:], 0.0)
         nc.vector.memset(w0s_raw[:].bitcast(I32), 0)
         nc.vector.memset(w1s[:].rearrange("p g n -> p (g n)").bitcast(I32), 0)
         nc.vector.memset(warm[:], 0.0)
@@ -105,10 +111,10 @@ def tile_spn_w4_kernel(tc, x_bytes, x_scale, w0_words, w0_scales, w1_words, w1_s
                 in_=w0_raw[:, 1024 * g : 1024 * (g + 1)].rearrange("p (m t b) -> p t m b", t=4, b=2),
             )
 
-        def permute_scales(g):
-            nc.vector.tensor_copy(
-                out=w0s_perm[:, 512 * g : 512 * (g + 1)].rearrange("p (t m) -> p t m", t=4),
-                in_=w0s_raw[:, 512 * g : 512 * (g + 1)].rearrange("p (m t) -> p t m", t=4),
+        def permute_scales(engine, g, t0, t1):
+            engine.tensor_copy(
+                out=w0s_perm[:, 512 * g : 512 * (g + 1)].rearrange("p (t m) -> p t m", t=4)[:, t0:t1],
+                in_=w0s_raw[:, 512 * g : 512 * (g + 1)].rearrange("p (m t) -> p t m", t=4)[:, t0:t1],
             )
 
         def x_mult(c, j):
@@ -119,7 +125,7 @@ def tile_spn_w4_kernel(tc, x_bytes, x_scale, w0_words, w0_scales, w1_words, w1_s
         def x_cast(c, j):
             t = work.tile([P, X], BF16, name="xv", bufs=8, align_bytes=64)
             xv[c, j] = t
-            (nc.scalar.copy if CE else nc.vector.tensor_copy)(out=t[:], in_=xb[c][:, j, :].bitcast(FP8))
+            (nc.scalar.copy if c or CE else nc.vector.tensor_copy)(out=t[:], in_=xb[c][:, j, :].bitcast(FP8))
 
         def x_scale_out(c, j):
             if j == 0:
@@ -241,13 +247,12 @@ def tile_spn_w4_kernel(tc, x_bytes, x_scale, w0_words, w0_scales, w1_words, w1_s
         last = n_chunks - 1
         tail = {}
 
-        def open_last():
-            for j in range(CHUNKS[last]):
-                for half in range(2):
-                    tag, bufs = ("xo", 3) if j == 0 else ("z", 5)
-                    o = psum.tile([P, P], F32, name="tail", tag=tag, bufs=bufs)
-                    tail[j, half] = o
-                    pass2(o[:], last, j, half, True, range(G - 1), False)
+        def open_last(j):
+            for half in range(2):
+                tag, bufs = ("xo", 3) if j == 0 else ("z", 5)
+                o = psum.tile([P, P], F32, name="tail", tag=tag, bufs=bufs)
+                tail[j, half] = o
+                pass2(o[:], last, j, half, True, range(G - 1), False)
 
         def close_last(j):
             for half in range(2):
@@ -259,6 +264,17 @@ def tile_spn_w4_kernel(tc, x_bytes, x_scale, w0_words, w0_scales, w1_words, w1_s
                 cols = slice(half * P, (half + 1) * P)
                 nc.vector.tensor_tensor(out=res[:, cols], in0=tail[j, half][:], in1=bias_o[:, cols], op=ADD)
             nc.sync.dma_start(out=out_view[:, first[last] + j, :], in_=res[:])
+
+        def spread_scales():
+            spread = psum.tile([P, 4, P], F32, name="spread", tag="xo", bufs=3)
+            for m in range(4):
+                nc.tensor.transpose(spread[:, m, :], xs_col[:, m : m + 1].to_broadcast([P, P]), ident[:])
+            nc.scalar.copy(out=xs[:].rearrange("p (n m) -> p n m", m=4), in_=spread[:].rearrange("p m n -> p n m"))
+
+        def dummies(k):
+            d = psum.tile([P, 512], F32, name="z", bufs=5)
+            for i in range(k):
+                nc.tensor.matmul(d[:], lhsT=zeros[:, :P], rhs=zeros[:], start=True, stop=True)
 
         n_units = len(UNITS)
         vec, mid, ten = {}, {}, {}
@@ -274,32 +290,40 @@ def tile_spn_w4_kernel(tc, x_bytes, x_scale, w0_words, w0_scales, w1_words, w1_s
         pairs = [(r + 1) // 2 for r in CHUNKS]
         for g in range(1, G):
             put(vec, PERM[g], permute_codes, g)
-            put(vec, PERM[g], permute_scales, g)
         for c in range(1, n_chunks):
             for j in range(CHUNKS[c]):
-                put(vec, XM[c][j], x_mult, c, j)
+                put(vec, XM[c][j], x_scale_out if c in SC else x_mult, c, j)
             for pair in range(pairs[c]):
-                put(ten, XT[c], x_transpose, c, pair)
-                put(ten, XT[c], x_copy, c, pair)
+                if c not in SC:
+                    put(ten, XT[c], x_transpose, c, pair)
+                    put(ten, XT[c], x_copy, c, pair)
             put(mid, XQ[c], x_quantize, c)
         for c in range(last):
             for i in range(pairs[c]):
                 k = min(2, CHUNKS[c] - 2 * i)
                 put(ten, S2[c][i], stage2, c, 2 * i, k)
                 put(vec if c == last - 1 else mid, S2[c][i] + 1, finish, c, 2 * i, k)
-        put(ten, n_units, open_last)
+        for j in range(CHUNKS[last]):
+            put(ten, OL[j], open_last, j)
+        put(ten, SP, spread_scales)
 
-        for j in range(CHUNKS[0]):
-            x_cast(0, j)
+        dummies(WARM[0])
+        for c in SC:
+            for j in range(CHUNKS[c]):
+                x_cast(c, j)
         x_transpose(0, 0)
-        spread = psum.tile([P, 4, P], F32, name="spread", tag="xo", bufs=3)
-        for m in range(4):
-            nc.tensor.transpose(spread[:, m, :], xs_col[:, m : m + 1].to_broadcast([P, P]), ident[:])
-        nc.scalar.copy(out=xs[:].rearrange("p (n m) -> p n m", m=4), in_=spread[:].rearrange("p m n -> p n m"))
+        for c in SC[1:]:
+            for pair in range(pairs[c]):
+                put(ten, XT[c], x_transpose, c, pair)
+        if WARM[1]:
+            dummies(WARM[1])
         permute_codes(0)
         for j in range(CHUNKS[0]):
             x_scale_out(0, j)
-        permute_scales(0)
+        permute_scales(nc.vector, 0, 0, 4)
+        for g in range(1, G):
+            for t in range(4):
+                permute_scales(nc.gpsimd, g, t, t + 1)
         x_quantize(0)
         run(vec, -2)
         run(vec, -1)

@@ -23,19 +23,20 @@ FLOPS = 2 * B * X * N + 2 * B * H * OS
 
 CHUNKS = (2, 4, 4, 4, 2)
 UNITS = tuple((c, g) for c in range(5) for g in range(4))
-SHARE = ((48, 48, 48, 48), (0, 0, 0, 0), (0, 0, 0, 0), (0, 0, 0, 0), (48, 48, 48, 48))
-VE = ((3, 3),)
+SHARE = ((48, 32, 32, 32), (0, 0, 0, 0), (0, 0, 0, 0), (0, 0, 0, 0), (0, 32, 64, 96))
+VE = ()
 CE = 0
 VX = ()
 SC = (0, 1)
+HV = (2, 2, 2, 2, 2)
 SP = 1
 OL = (20, 20)
-WARM = (5, 3)
+WARM = (4, 3)
 XM = ((), (0, 0, 0, 0), (2, 2, 3, 3), (6, 6, 7, 7), (10, 10))
 XT = (0, 0, 5, 9, 13)
 XQ = (0, 1, 6, 10, 14)
 S2 = ((6,), (10, 11), (14, 15), (18, 19))
-PERM = (-2, -2, -2, -1)
+PERM = (-2, -2, -1, 0)
 
 
 def tile_spn_w4_kernel(tc, x_bytes, x_scale, w0_words, w0_scales, w1_words, w1_scales, biases, out):
@@ -71,22 +72,23 @@ def tile_spn_w4_kernel(tc, x_bytes, x_scale, w0_words, w0_scales, w1_words, w1_s
         zeros = keep.tile([P, 512], BF16, name="zeros")
         nc.vector.memset(zeros[:], 0.0)
         nc.vector.memset(w0s_raw[:].bitcast(I32), 0)
-        nc.vector.memset(w1s[:].rearrange("p g n -> p (g n)").bitcast(I32), 0)
         nc.vector.memset(warm[:], 0.0)
+        nc.vector.memset(w1s[:].rearrange("p g n -> p (g n)").bitcast(I32), 0)
         make_identity(nc, ident[:])
 
         def load_x(c):
             nc.sync.dma_start(out=xb[c][:], in_=x_view[:, first[c] : first[c] + CHUNKS[c], :])
 
+        nc.scalar.activation(out=warm[:], in_=warm[:], func=RELU)
         load_x(0)
         nc.sync.dma_start(out=xs_col[:], in_=x_scale.rearrange("o (n m) -> n (o m)", m=4))
         nc.sync.dma_start(out=w0_raw[:, 0:1024], in_=w0_words[0, :, 0:1024])
-        load_x(1)
         for q in range(4):
             nc.sync.dma_start(
                 out=w0s_raw[32 * q : 32 * q + 4, :].bitcast(I32),
                 in_=w0_scales[0, 4 * q : 4 * q + 4, :].bitcast(I32),
             )
+        load_x(1)
         nc.scalar.dma_start(out=bias_h[:], in_=biases[0:H].rearrange("(g p t) -> p g t", g=G, p=P, t=4))
         nc.sync.dma_start(out=w0_raw[:, 1024:2048], in_=w0_words[0, :, 1024:2048])
         nc.sync.dma_start(out=w0_raw[:, 2048:4608], in_=w0_words[0, :, 2048:4608])
@@ -99,7 +101,6 @@ def tile_spn_w4_kernel(tc, x_bytes, x_scale, w0_words, w0_scales, w1_words, w1_s
         for c in range(2, n_chunks):
             load_x(c)
         nc.sync.dma_start(out=bias_o[:], in_=biases[H:N].partition_broadcast(P))
-        nc.scalar.activation(out=warm[:], in_=warm[:], func=RELU)
 
         xv, xg, xq, xqs = {}, {}, {}, {}
         xt = {}
@@ -286,10 +287,11 @@ def tile_spn_w4_kernel(tc, x_bytes, x_scale, w0_words, w0_scales, w1_words, w1_s
             for f, args in table.get(s, []):
                 f(*args)
 
-        halves = [1 if r == 1 else 2 for r in CHUNKS]
+        halves = [HV[c] for c in range(n_chunks)]
         pairs = [(r + 1) // 2 for r in CHUNKS]
         for g in range(1, G):
             put(vec, PERM[g], permute_codes, g)
+            put(vec, PERM[g], permute_scales, nc.vector, g, 0, 4)
         for c in range(1, n_chunks):
             for j in range(CHUNKS[c]):
                 put(vec, XM[c][j], x_scale_out if c in SC else x_mult, c, j)
@@ -321,9 +323,6 @@ def tile_spn_w4_kernel(tc, x_bytes, x_scale, w0_words, w0_scales, w1_words, w1_s
         for j in range(CHUNKS[0]):
             x_scale_out(0, j)
         permute_scales(nc.vector, 0, 0, 4)
-        for g in range(1, G):
-            for t in range(4):
-                permute_scales(nc.gpsimd, g, t, t + 1)
         x_quantize(0)
         run(vec, -2)
         run(vec, -1)

from contextlib import ExitStack

import concourse.mybir as mybir
from concourse.masks import make_identity

F32 = mybir.dt.float32
BF16 = mybir.dt.bfloat16
U32 = mybir.dt.uint32
I32 = mybir.dt.int32
U8 = mybir.dt.uint8
FP8 = mybir.dt.float8_e4m3fn
FP8X4 = mybir.dt.float8_e4m3fn_x4
FP4X4 = mybir.dt.float4_e2m1fn_x4
RELU = mybir.ActivationFunctionType.Relu
MULT = mybir.AluOpType.mult
ADD = mybir.AluOpType.add

P = 128
B, X, N, OS = 2048, 512, 2304, 256
H = N - OS
G = H // 512
FLOPS = 2 * B * X * N + 2 * B * H * OS

CHUNKS = (2, 4, 4, 4, 2)
UNITS = tuple((c, g) for c in range(5) for g in range(4))
SHARE = ((48, 32, 32, 32), (0, 0, 0, 0), (0, 0, 0, 0), (0, 0, 0, 0), (0, 32, 64, 96))
VE = ()
CE = 0
VX = ()
SC = (0, 1)
HV = (2, 2, 2, 2, 2)
SP = 1
OL = (20, 20)
WARM = (4, 3)
XM = ((), (0, 0, 0, 0), (2, 2, 3, 3), (6, 6, 7, 7), (10, 10))
XT = (0, 0, 5, 9, 13)
XQ = (0, 1, 6, 10, 14)
S2 = ((6,), (10, 11), (14, 15), (18, 19))
PERM = (-2, -2, -1, 0)


def tile_spn_w4_kernel(tc, x_bytes, x_scale, w0_words, w0_scales, w1_words, w1_scales, biases, out):
    nc = tc.nc
    n_chunks = len(CHUNKS)
    first = [sum(CHUNKS[:c]) for c in range(n_chunks)]
    x_view = x_bytes.rearrange("(p j) k -> p j k", j=B // P)
    out_view = out.rearrange("(p j) n -> p j n", j=B // P)

    with ExitStack() as ctx:
        keep = ctx.enter_context(tc.tile_pool(name="keep", bufs=1))
        work = ctx.enter_context(tc.tile_pool(name="work", bufs=4))
        psum = ctx.enter_context(tc.psum_pool(name="psum", bufs=5))
        ctx.enter_context(tc.manual_schedule())

        ident = keep.tile([P, P], F32, name="ident")
        xs = keep.tile([P, X], F32, name="xs")
        w0_raw = keep.tile([P, 2 * N], U8, name="w0_raw", align_bytes=64)
        w0s_raw = keep.tile([P, N], U8, name="w0s_raw", align_bytes=64)
        w0_perm = keep.tile([P, 2 * H], U8, name="w0_perm", align_bytes=64)
        w0s_perm = keep.tile([P, H], U8, name="w0s_perm", align_bytes=64)
        w1 = keep.tile([P, G, 2 * OS], U8, name="w1", align_bytes=64)
        w1s = keep.tile([P, G, OS], U8, name="w1s", align_bytes=64)
        bias_h = keep.tile([P, G, 4], BF16, name="bias_h")
        bias_o = keep.tile([P, OS], BF16, name="bias_o")
        xs_col = keep.tile([P, 4], F32, name="xs_col")
        warm = keep.tile([P, 1], F32, name="warm")
        xb = []
        for c in range(n_chunks):
            xb_c = keep.tile([P, CHUNKS[c], X], U8, name="xbytes%d" % c, align_bytes=64)
            xb.append(xb_c)

        zeros = keep.tile([P, 512], BF16, name="zeros")
        nc.vector.memset(zeros[:], 0.0)
        nc.vector.memset(w0s_raw[:].bitcast(I32), 0)
        nc.vector.memset(warm[:], 0.0)
        nc.vector.memset(w1s[:].rearrange("p g n -> p (g n)").bitcast(I32), 0)
        make_identity(nc, ident[:])

        def load_x(c):
            nc.sync.dma_start(out=xb[c][:], in_=x_view[:, first[c] : first[c] + CHUNKS[c], :])

        nc.scalar.activation(out=warm[:], in_=warm[:], func=RELU)
        load_x(0)
        nc.sync.dma_start(out=xs_col[:], in_=x_scale.rearrange("o (n m) -> n (o m)", m=4))
        nc.sync.dma_start(out=w0_raw[:, 0:1024], in_=w0_words[0, :, 0:1024])
        for q in range(4):
            nc.sync.dma_start(
                out=w0s_raw[32 * q : 32 * q + 4, :].bitcast(I32),
                in_=w0_scales[0, 4 * q : 4 * q + 4, :].bitcast(I32),
            )
        load_x(1)
        nc.scalar.dma_start(out=bias_h[:], in_=biases[0:H].rearrange("(g p t) -> p g t", g=G, p=P, t=4))
        nc.sync.dma_start(out=w0_raw[:, 1024:2048], in_=w0_words[0, :, 1024:2048])
        nc.sync.dma_start(out=w0_raw[:, 2048:4608], in_=w0_words[0, :, 2048:4608])
        nc.sync.dma_start(out=w1[:], in_=w1_words.rearrange("g p n -> p g n"))
        for q in range(4):
            nc.sync.dma_start(
                out=w1s[32 * q : 32 * q + 4].bitcast(I32),
                in_=w1_scales[:, 4 * q : 4 * q + 4, :].rearrange("g r n -> r g n").bitcast(I32),
            )
        for c in range(2, n_chunks):
            load_x(c)
        nc.sync.dma_start(out=bias_o[:], in_=biases[H:N].partition_broadcast(P))

        xv, xg, xq, xqs = {}, {}, {}, {}
        xt = {}
        hp, hg, hq, hqs, acc = {}, {}, {}, {}, {}

        def permute_codes(g):
            nc.vector.tensor_copy(
                out=w0_perm[:, 1024 * g : 1024 * (g + 1)].rearrange("p (t m b) -> p t m b", t=4, b=2),
                in_=w0_raw[:, 1024 * g : 1024 * (g + 1)].rearrange("p (m t b) -> p t m b", t=4, b=2),
            )

        def permute_scales(engine, g, t0, t1):
            engine.tensor_copy(
                out=w0s_perm[:, 512 * g : 512 * (g + 1)].rearrange("p (t m) -> p t m", t=4)[:, t0:t1],
                in_=w0s_raw[:, 512 * g : 512 * (g + 1)].rearrange("p (m t) -> p t m", t=4)[:, t0:t1],
            )

        def x_mult(c, j):
            t = work.tile([P, X], BF16, name="xv", bufs=8, align_bytes=64)
            xv[c, j] = t
            nc.vector.tensor_tensor(out=t[:], in0=xb[c][:, j, :].bitcast(FP8), in1=xs[:], op=MULT)

        def x_cast(c, j):
            t = work.tile([P, X], BF16, name="xv", bufs=8, align_bytes=64)
            xv[c, j] = t
            (nc.scalar.copy if c or CE else nc.vector.tensor_copy)(out=t[:], in_=xb[c][:, j, :].bitcast(FP8))

        def x_scale_out(c, j):
            if j == 0:
                xg[c] = work.tile([P, 2048], BF16, name="xg", bufs=2, align_bytes=64)
            nc.vector.tensor_tensor(
                out=xg[c][:, 512 * j : 512 * (j + 1)].rearrange("p (r u e) -> p r u e", u=2, e=2),
                in0=xt[c, j // 2][:, j % 2].rearrange("p u r -> p (u r)").bitcast(BF16).rearrange("p (u r e) -> p r u e", u=2, e=2),
                in1=xs_col[:].rearrange("p (o u e) -> p o u e", o=1, u=2).to_broadcast([P, P, 2, 2]),
                op=MULT,
            )

        def x_transpose(c, pair):
            t = psum.tile([P, 2, 2, P], F32, name="xt", tag="xo", bufs=3)
            xt[c, pair] = t
            for jj in range(min(2, CHUNKS[c] - 2 * pair)):
                words = xv[c, 2 * pair + jj][:].bitcast(F32)
                for u in range(2):
                    nc.tensor.transpose(t[:, jj, u, :], words[:, u : X // 2 : 2], ident[:])

        def x_copy(c, pair):
            if pair == 0:
                xg[c] = work.tile([P, 2048], BF16, name="xg", bufs=2, align_bytes=64)
            k = min(2, CHUNKS[c] - 2 * pair)
            move = nc.vector.tensor_copy if (c, pair) in VX else nc.scalar.copy
            move(
                out=xg[c][:, 1024 * pair : 1024 * pair + 512 * k].bitcast(F32).rearrange("p (j r u) -> p j r u", j=k, u=2),
                in_=xt[c, pair][:, :k].rearrange("p j u r -> p j r u"),
            )

        def x_quantize(c):
            n = CHUNKS[c] * P
            xq[c] = work.tile([P, 512], U32, name="xq", bufs=n_chunks, align_bytes=64)
            xqs[c] = work.tile([P, 512], U8, name="xqs", bufs=n_chunks, align_bytes=64)
            nc.vector.quantize_mx(out=xq[c][:, :n].bitcast(FP8X4), scales=xqs[c][:, :n], in_=xg[c][:, : 4 * n])

        def stage1(c, g):
            n = CHUNKS[c] * P
            h = work.tile([P, 4, 512], BF16, name="hp", bufs=4, align_bytes=64)
            hp[c, g] = h
            for t in range(4):
                z = psum.tile([P, 512], F32, name="z", bufs=5)
                m0 = 512 * g + P * t
                nc.tensor.matmul_mx(
                    out=z[:, :n],
                    lhsT=w0_perm[:, 2 * m0 : 2 * (m0 + P)].bitcast(FP4X4),
                    lhsT_scale=w0s_perm[:, m0 : m0 + P],
                    rhs=xq[c][:, :n].bitcast(FP8X4),
                    rhs_scale=xqs[c][:, :n],
                    start=True,
                    stop=True,
                )
                if t == 3 and (c, g) in VE:
                    nc.vector.tensor_scalar(out=h[:, t, :n], in0=z[:, :n], scalar1=bias_h[:, g, t : t + 1], scalar2=0.0, op0=ADD, op1=mybir.AluOpType.max)
                else:
                    nc.scalar.activation(out=h[:, t, :n], in_=z[:, :n], func=RELU, bias=bias_h[:, g, t : t + 1])
            hg[c, g] = work.tile([P, 2048], BF16, name="hg", bufs=4, align_bytes=64)
            weave(nc.scalar.copy, c, g, n - SHARE[c][g], n)

        def weave(engine_copy, c, g, a, b):
            if b > a:
                engine_copy(
                    out=hg[c, g][:, 4 * a : 4 * b].rearrange("p (c i t) -> p c t i", t=4, i=4),
                    in_=hp[c, g][:, :, a:b].rearrange("p t (c i) -> p c t i", i=4),
                )

        def h_quantize(c, g, half):
            n = CHUNKS[c] * P // halves[c]
            if half == 0:
                hq[c, g] = work.tile([P, 512], U32, name="hq", bufs=12, align_bytes=64)
                hqs[c, g] = work.tile([P, 512], U8, name="hqs", bufs=12, align_bytes=64)
            a = half * n
            nc.vector.quantize_mx(
                out=hq[c, g][:, a : a + n].bitcast(FP8X4),
                scales=hqs[c, g][:, a : a + n],
                in_=hg[c, g][:, 4 * a : 4 * (a + n)],
            )

        def pass2(dst, c, j, half, opens, groups, closes):
            cols = slice(j * P, (j + 1) * P)
            n0 = H + half * P
            if opens:
                nc.tensor.matmul_mx(
                    out=dst,
                    lhsT=xq[c][:, cols].bitcast(FP8X4),
                    lhsT_scale=xqs[c][:, cols],
                    rhs=w0_raw[:, 2 * n0 : 2 * (n0 + P)].bitcast(FP4X4),
                    rhs_scale=w0s_raw[:, n0 : n0 + P],
                    start=True,
                    stop=False,
                )
            for g in groups:
                nc.tensor.matmul_mx(
                    out=dst,
                    lhsT=hq[c, g][:, cols].bitcast(FP8X4),
                    lhsT_scale=hqs[c, g][:, cols],
                    rhs=w1[:, g, 2 * half * P : 2 * (half + 1) * P].bitcast(FP4X4),
                    rhs_scale=w1s[:, g, half * P : (half + 1) * P],
                    start=False,
                    stop=(closes and g == groups[-1]),
                )

        def stage2(c, j0, count):
            o = psum.tile([P, 2, OS], F32, name="o", tag="xo", bufs=3)
            acc[c, j0] = o
            for jj in range(count):
                for half in range(2):
                    pass2(o[:, jj, half * P : (half + 1) * P], c, j0 + jj, half, True, range(G), True)

        def finish(c, j0, count):
            res = work.tile([P, 2, OS], F32, name="res", bufs=4)
            nc.vector.tensor_tensor(
                out=res[:, :count, :],
                in0=acc[c, j0][:, :count, :],
                in1=bias_o[:].unsqueeze(1).to_broadcast([P, count, OS]),
                op=ADD,
            )
            nc.sync.dma_start(out=out_view[:, first[c] + j0 : first[c] + j0 + count, :], in_=res[:, :count, :])

        last = n_chunks - 1
        tail = {}

        def open_last(j):
            for half in range(2):
                tag, bufs = ("xo", 3) if j == 0 else ("z", 5)
                o = psum.tile([P, P], F32, name="tail", tag=tag, bufs=bufs)
                tail[j, half] = o
                pass2(o[:], last, j, half, True, range(G - 1), False)

        def close_last(j):
            for half in range(2):
                pass2(tail[j, half][:], last, j, half, False, (G - 1,), True)

        def finish_last(j):
            res = work.tile([P, OS], F32, name="tail_res", bufs=2)
            for half in range(2):
                cols = slice(half * P, (half + 1) * P)
                nc.vector.tensor_tensor(out=res[:, cols], in0=tail[j, half][:], in1=bias_o[:, cols], op=ADD)
            nc.sync.dma_start(out=out_view[:, first[last] + j, :], in_=res[:])

        def spread_scales():
            spread = psum.tile([P, 4, P], F32, name="spread", tag="xo", bufs=3)
            for m in range(4):
                nc.tensor.transpose(spread[:, m, :], xs_col[:, m : m + 1].to_broadcast([P, P]), ident[:])
            nc.scalar.copy(out=xs[:].rearrange("p (n m) -> p n m", m=4), in_=spread[:].rearrange("p m n -> p n m"))

        def dummies(k):
            d = psum.tile([P, 512], F32, name="z", bufs=5)
            for i in range(k):
                nc.tensor.matmul(d[:], lhsT=zeros[:, :P], rhs=zeros[:], start=True, stop=True)

        n_units = len(UNITS)
        vec, mid, ten = {}, {}, {}

        def put(table, s, f, *args):
            table.setdefault(s, []).append((f, args))

        def run(table, s):
            for f, args in table.get(s, []):
                f(*args)

        halves = [HV[c] for c in range(n_chunks)]
        pairs = [(r + 1) // 2 for r in CHUNKS]
        for g in range(1, G):
            put(vec, PERM[g], permute_codes, g)
            put(vec, PERM[g], permute_scales, nc.vector, g, 0, 4)
        for c in range(1, n_chunks):
            for j in range(CHUNKS[c]):
                put(vec, XM[c][j], x_scale_out if c in SC else x_mult, c, j)
            for pair in range(pairs[c]):
                if c not in SC:
                    put(ten, XT[c], x_transpose, c, pair)
                    put(ten, XT[c], x_copy, c, pair)
            put(mid, XQ[c], x_quantize, c)
        for c in range(last):
            for i in range(pairs[c]):
                k = min(2, CHUNKS[c] - 2 * i)
                put(ten, S2[c][i], stage2, c, 2 * i, k)
                put(vec if c == last - 1 else mid, S2[c][i] + 1, finish, c, 2 * i, k)
        for j in range(CHUNKS[last]):
            put(ten, OL[j], open_last, j)
        put(ten, SP, spread_scales)

        dummies(WARM[0])
        for c in SC:
            for j in range(CHUNKS[c]):
                x_cast(c, j)
        x_transpose(0, 0)
        for c in SC[1:]:
            for pair in range(pairs[c]):
                put(ten, XT[c], x_transpose, c, pair)
        if WARM[1]:
            dummies(WARM[1])
        permute_codes(0)
        for j in range(CHUNKS[0]):
            x_scale_out(0, j)
        permute_scales(nc.vector, 0, 0, 4)
        x_quantize(0)
        run(vec, -2)
        run(vec, -1)

        for s in range(n_units + 1):
            if s < n_units:
                stage1(*UNITS[s])
            if s > 0:
                c, g = UNITS[s - 1]
                n = CHUNKS[c] * P
                cut = n // halves[c]
                end = n - SHARE[c][g]
                weave(nc.vector.tensor_copy, c, g, 0, min(cut, end))
                weave(nc.vector.tensor_copy, c, g, cut, end)
            run(mid, s)
            if s > 0:
                h_quantize(c, g, 0)
                if halves[c] == 2:
                    h_quantize(c, g, 1)
            run(ten, s)
            run(vec, s)
        for j in range(CHUNKS[last]):
            close_last(j)
            finish_last(j)
